import numpy as np
import ml_dtypes


def mxq(x, axis, fmt="e4m3"):
    dtype, down = {"e4m3": (ml_dtypes.float8_e4m3fn, 7), "e5m2": (ml_dtypes.float8_e5m2, 14)}[fmt]
    v = np.moveaxis(np.asarray(x, np.float32).astype(ml_dtypes.bfloat16).astype(np.float64), axis, -1)
    blocks = v.reshape(v.shape[:-1] + (-1, 32))
    amax = np.abs(blocks).max(-1, keepdims=True)
    byte = np.maximum(np.where(amax > 0, np.frexp(amax)[1] - 1 + 127, 0) - down, 1)
    scale = np.exp2(byte - 127.0)
    codes = (blocks / scale).astype(np.float32).astype(dtype).astype(np.float64)
    return np.moveaxis((codes * scale).reshape(v.shape), -1, axis)


BF16 = ml_dtypes.bfloat16


def bf(x):
    return np.asarray(x, np.float32).astype(BF16)


def f64(x):
    return np.asarray(x).astype(np.float64)


B, CIN, H, W, D, K, NCLASS, WIN = 2, 2048, 33, 33, 128, 128, 1000, 32
P = (H - WIN + 1) * (W - WIN + 1)
N = WIN * WIN


def setup_inputs():
    return {"x_pat": bf(np.maximum(np.random.standard_normal((B, P, N, D)), 0.0) * 3.4 / np.sqrt(D)),
            "codewords": bf(np.random.uniform(-1.0, 1.0, (K, D)) * 2.4 / np.sqrt(D)),
            "scale": bf(-np.random.uniform(0.0, 1.0, K))}


def reference(x_pat, codewords, scale):
    xf = f64(x_pat)
    cw = f64(codewords)
    x2 = np.sum(xf * xf, -1)
    c2 = np.sum(cw * cw, -1)
    xc = f64(x_pat) @ f64(codewords).T
    dist = x2[..., None] - 2.0 * xc + c2
    z = f64(scale) * dist
    ez = np.exp(z - z.max(-1, keepdims=True))
    A = ez / ez.sum(-1, keepdims=True)
    agg = mxq(A, 2, "e4m3").transpose(0, 1, 3, 2) @ mxq(xf, 2, "e4m3")
    E = agg - A.sum(2)[..., None] * cw
    e = E.reshape(B, P, K * D)
    e = e / np.maximum(np.sqrt(np.sum(e * e, -1, keepdims=True)), 1e-12)
    return e.sum(1)

@@ -1,0 +1,261 @@
+from contextlib import ExitStack
+
+import concourse.mybir as mybir
+from concourse.masks import make_identity
+
+F32 = mybir.dt.float32
+BF16 = mybir.dt.bfloat16
+U32 = mybir.dt.uint32
+U8 = mybir.dt.uint8
+FP8X4 = mybir.dt.float8_e4m3fn_x4
+ALU = mybir.AluOpType
+ACT = mybir.ActivationFunctionType
+AX = mybir.AxisListType
+
+P = 128
+PACK = 4
+IMAGES = 2
+PATCHES = 4
+PIXELS = 1024
+D = 128
+K = 128
+HALVES = PIXELS // (P * PACK)
+
+FLOPS = 2 * 2 * IMAGES * PATCHES * PIXELS * K * D
+
+
+def tile_att_patch_net_pa_s_kernel(tc, x_pat, codewords, scale, out):
+    nc = tc.nc
+    n_patches = IMAGES * PATCHES
+    n_units = n_patches * HALVES
+    with ExitStack() as ctx:
+        consts = ctx.enter_context(tc.tile_pool(name="consts", bufs=1))
+        work = ctx.enter_context(tc.tile_pool(name="work", bufs=3))
+        keep = ctx.enter_context(tc.tile_pool(name="keep", bufs=4))
+        ps_t = ctx.enter_context(tc.psum_pool(name="ps_t", bufs=2))
+        ps_u = ctx.enter_context(tc.psum_pool(name="ps_u", bufs=4))
+        ps_out = ctx.enter_context(tc.psum_pool(name="ps_out", bufs=2))
+        ctx.enter_context(tc.manual_schedule())
+
+        cw = consts.tile([K, D], BF16)
+        nc.scalar.dma_start(out=cw[:], in_=codewords)
+        s_rows = consts.tile([P, K], BF16)
+        nc.vector.memset(s_rows[:], 0.0)
+        nc.scalar.dma_start(out=s_rows[0:1, :], in_=scale.unsqueeze(0))
+        raws = []
+        for h in range(n_units):
+            g, c = divmod(h, HALVES)
+            raw = consts.tile([P, PACK, D], BF16, name="raw%d" % h)
+            rows = x_pat[g // PATCHES, g % PATCHES, c * P * PACK : (c + 1) * P * PACK, :]
+            nc.sync.dma_start(out=raw[:], in_=rows.rearrange("(p j) d -> p j d", j=PACK))
+            raws.append(raw)
+
+        ident = consts.tile([P, P], BF16)
+        make_identity(nc, ident[:])
+        ident_f = consts.tile([P, P], F32)
+        make_identity(nc, ident_f[:])
+        ones_bf = consts.tile([P, P], BF16)
+        nc.vector.memset(ones_bf[:], 1.0)
+        ones_f = consts.tile([P, P], F32)
+        nc.vector.memset(ones_f[:], 1.0)
+
+        cwT_ps = ps_t.tile([D, K], BF16, tag="xT_ps")
+        nc.tensor.transpose(cwT_ps[:], cw[:], ident[:])
+        cwT_m2 = consts.tile([D, K], BF16)
+        nc.vector.tensor_scalar_mul(out=cwT_m2[:], in0=cwT_ps[:], scalar1=-2.0)
+
+        c2 = consts.tile([K, 1], F32)
+        cw_junk = consts.tile([K, D], F32)
+        nc.scalar.activation(out=cw_junk[:], in_=cw[:], func=ACT.Square, accum_out=c2[:])
+        c2_rows = consts.tile([K, P], F32)
+        nc.vector.tensor_copy(out=c2_rows[:], in_=c2[:, 0:1].to_broadcast([K, P]))
+
+        s_ps = ps_u.tile([P, K], F32, tag="u_ps")
+        nc.tensor.matmul(s_ps[:], lhsT=ones_bf[:], rhs=s_rows[:], start=True, stop=True)
+        neg_s_all = consts.tile([P, K], F32)
+        nc.vector.tensor_scalar_mul(out=neg_s_all[:], in0=s_ps[:], scalar1=-1.0)
+
+        resid = consts.tile([K, n_patches, D], F32)
+        ssq = consts.tile([K, n_patches], F32)
+
+        live = {}
+
+        def transposes(h):
+            raw = raws[h]
+            x2 = keep.tile([P, PACK], F32)
+            sq_junk = work.tile([P, PACK, D], BF16)
+            for j in range(PACK):
+                nc.scalar.activation(
+                    out=sq_junk[:, j, :], in_=raw[:, j, :], func=ACT.Square, accum_out=x2[:, j : j + 1]
+                )
+            xT_ps = ps_t.tile([D, PACK, P], BF16)
+            for j in range(PACK):
+                nc.tensor.transpose(xT_ps[:, j, :], raw[:, j, :], ident[:])
+            xT = work.tile([D, PACK, P], BF16)
+            nc.scalar.copy(out=xT[:], in_=xT_ps[:])
+            live[("x2", h)] = x2
+            live[("xT", h)] = xT
+
+        def products(h):
+            u_ps = ps_u.tile([P, PACK, K], F32)
+            for j in range(PACK):
+                nc.tensor.matmul(u_ps[:, j, :], lhsT=live[("xT", h)][:, j, :], rhs=cwT_m2[:], start=True, stop=False)
+                nc.tensor.matmul(
+                    u_ps[:, j, :], lhsT=c2_rows[:], rhs=ident_f[:], is_transpose=True, start=False, stop=True
+                )
+            live[("u", h)] = u_ps
+
+        def distances(h):
+            neg_z = work.tile([P, PACK, K], F32)
+            for j in range(PACK):
+                nc.vector.scalar_tensor_tensor(
+                    out=neg_z[:, j, :],
+                    in0=live[("u", h)][:, j, :],
+                    scalar=live[("x2", h)][:, j : j + 1],
+                    in1=neg_s_all[:],
+                    op0=ALU.add,
+                    op1=ALU.mult,
+                )
+            low = keep.tile([P, PACK], F32)
+            nc.vector.tensor_reduce(out=low[:], in_=neg_z[:], axis=AX.X, op=ALU.min)
+            live[("neg_z", h)] = neg_z
+            live[("low", h)] = low
+
+        def exps(h):
+            e = work.tile([P, PACK, K], F32)
+            esum = keep.tile([P, PACK], F32)
+            for j in range(PACK):
+                nc.scalar.activation(
+                    out=e[:, j, :],
+                    in_=live[("neg_z", h)][:, j, :],
+                    func=ACT.Exp,
+                    bias=live[("low", h)][:, j : j + 1],
+                    scale=-1.0,
+                    accum_out=esum[:, j : j + 1],
+                )
+            live[("e", h)] = e
+            live[("esum", h)] = esum
+
+        def normalise(h):
+            g, c = divmod(h, HALVES)
+            e = live[("e", h)]
+            rinv = keep.tile([P, PACK], F32)
+            nc.vector.reciprocal(out=rinv[:], in_=live[("esum", h)][:])
+            if c == 0:
+                sums_ps = ps_out.tile([K, D + 1], F32, tag="sums")
+                live[("sums", g)] = sums_ps
+            for j in range(PACK):
+                nc.tensor.matmul(
+                    live[("sums", g)][:, D : D + 1],
+                    lhsT=e[:, j, :],
+                    rhs=rinv[:, j : j + 1],
+                    start=(c == 0 and j == 0),
+                    stop=(c == HALVES - 1 and j == PACK - 1),
+                )
+            a_grp = work.tile([P, K, PACK], BF16, align_bytes=64)
+            nc.vector.tensor_tensor(
+                out=a_grp[:],
+                in0=e[:].rearrange("p j k -> p k j"),
+                in1=rinv[:].unsqueeze(1).to_broadcast([P, K, PACK]),
+                op=ALU.mult,
+            )
+            live[("a_grp", h)] = a_grp
+
+        def regroup_x(h):
+            x_grp = keep.tile([P, D, PACK], BF16, align_bytes=64)
+            nc.vector.tensor_copy(out=x_grp[:], in_=raws[h][:].rearrange("p j d -> p d j"))
+            live[("x_grp", h)] = x_grp
+
+        def quantise(name, h):
+            codes = keep.tile([P, D], U32, align_bytes=64, tag=name + "_codes")
+            scales = keep.tile([P, D], U8, align_bytes=64, tag=name + "_scales")
+            nc.vector.quantize_mx(
+                out=codes[:].bitcast(FP8X4),
+                scales=scales[:],
+                in_=live[(name + "_grp", h)][:].rearrange("p w j -> p (w j)"),
+            )
+            live[(name + "_codes", h)] = codes
+            live[(name + "_scales", h)] = scales
+
+        def aggregate(g):
+            for c in range(HALVES):
+                h = g * HALVES + c
+                nc.tensor.matmul_mx(
+                    out=live[("sums", g)][:, 0:D],
+                    lhsT=live[("a_codes", h)][:].bitcast(FP8X4),
+                    lhsT_scale=live[("a_scales", h)][:],
+                    rhs=live[("x_codes", h)][:].bitcast(FP8X4),
+                    rhs_scale=live[("x_scales", h)][:],
+                    start=(c == 0),
+                    stop=(c == HALVES - 1),
+                )
+
+        def residual(g):
+            neg_asum = keep.tile([K, 1], F32)
+            nc.vector.tensor_scalar_mul(out=neg_asum[:], in0=live[("sums", g)][:, D : D + 1], scalar1=-1.0)
+            nc.vector.scalar_tensor_tensor(
+                out=resid[:, g, :],
+                in0=cw[:],
+                scalar=neg_asum[:, 0:1],
+                in1=live[("sums", g)][:, 0:D],
+                op0=ALU.mult,
+                op1=ALU.add,
+            )
+
+        def residual_norm(g):
+            e_junk = work.tile([K, D], F32)
+            nc.scalar.activation(out=e_junk[:], in_=resid[:, g, :], func=ACT.Square, accum_out=ssq[:, g : g + 1])
+
+        def unit(h):
+            return 0 <= h < n_units
+
+        for r in range(n_units + 5):
+            if unit(r):
+                transposes(r)
+            if unit(r - 1):
+                products(r - 1)
+            if unit(r - 2):
+                distances(r - 2)
+                exps(r - 2)
+            if unit(r - 3):
+                normalise(r - 3)
+            if unit(r - 2):
+                quantise("x", r - 2)
+            if unit(r):
+                regroup_x(r)
+            if unit(r - 5) and (r - 5) % HALVES == HALVES - 1:
+                residual((r - 5) // HALVES)
+            if unit(r - 3):
+                quantise("a", r - 3)
+            if unit(r - 3) and (r - 3) % HALVES == HALVES - 1:
+                aggregate((r - 3) // HALVES)
+            if unit(r - 5) and (r - 5) % HALVES == HALVES - 1:
+                residual_norm((r - 5) // HALVES)
+            if r - 2 == n_units - 1:
+                warm = consts.tile([P, 1], F32)
+                nc.scalar.activation(out=warm[:], in_=ones_f[:, 0:1], func=ACT.Sqrt)
+
+        tot_ps = ps_out.tile([P, n_patches], F32, tag="sums")
+        nc.tensor.matmul(tot_ps[:], lhsT=ones_f[:], rhs=ssq[:], start=True, stop=True)
+        norm = keep.tile([P, n_patches], F32)
+        nc.scalar.activation(out=norm[:], in_=tot_ps[:], func=ACT.Sqrt)
+        nc.vector.tensor_scalar_max(out=norm[:], in0=norm[:], scalar1=1e-12)
+        rnorm = keep.tile([P, n_patches], F32)
+        nc.vector.reciprocal(out=rnorm[:], in_=norm[:])
+        accs = [consts.tile([K, D], F32, name="acc%d" % b) for b in range(IMAGES)]
+        for t in range(PATCHES):
+            for b in range(IMAGES):
+                g = b * PATCHES + t
+                if t == 0:
+                    nc.vector.tensor_scalar_mul(out=accs[b][:], in0=resid[:, g, :], scalar1=rnorm[:, g : g + 1])
+                else:
+                    nc.vector.scalar_tensor_tensor(
+                        out=accs[b][:],
+                        in0=resid[:, g, :],
+                        scalar=rnorm[:, g : g + 1],
+                        in1=accs[b][:],
+                        op0=ALU.mult,
+                        op1=ALU.add,
+                    )
+        nc.sync.dma_start(out=out[0].rearrange("(k d) -> k d", d=D), in_=accs[0][:])
+        nc.scalar.dma_start(out=out[1].rearrange("(k d) -> k d", d=D), in_=accs[1][:])

@@ -75,6 +75,9 @@ def tile_att_patch_net_pa_s_kernel(tc, x_pat, codewords, scale, out):
         neg_s_all = consts.tile([P, K], F32)
         nc.vector.tensor_scalar_mul(out=neg_s_all[:], in0=s_ps[:], scalar1=-1.0)
 
+        neg_cw = consts.tile([K, D], BF16)
+        nc.vector.tensor_scalar_mul(out=neg_cw[:], in0=cw[:], scalar1=-1.0)
+
         resid = consts.tile([K, n_patches, D], F32)
         ssq = consts.tile([K, n_patches], F32)
 
@@ -136,30 +139,37 @@ def tile_att_patch_net_pa_s_kernel(tc, x_pat, codewords, scale, out):
             live[("e", h)] = e
             live[("esum", h)] = esum
 
-        def normalise(h):
-            g, c = divmod(h, HALVES)
-            e = live[("e", h)]
+        def reciprocals(h):
             rinv = keep.tile([P, PACK], F32)
             nc.vector.reciprocal(out=rinv[:], in_=live[("esum", h)][:])
+            live[("rinv", h)] = rinv
+
+        def normalise(h):
+            a = work.tile([P, PACK, K], F32)
+            for j in range(PACK):
+                nc.scalar.activation(
+                    out=a[:, j, :], in_=live[("e", h)][:, j, :], func=ACT.Copy, scale=live[("rinv", h)][:, j : j + 1]
+                )
+            live[("a", h)] = a
+
+        def round_a(h):
+            g, c = divmod(h, HALVES)
+            a = live[("a", h)]
+            a_grp = work.tile([P, K, PACK], BF16, align_bytes=64)
+            nc.vector.tensor_copy(out=a_grp[:], in_=a[:].rearrange("p j k -> p k j"))
+            live[("a_grp", h)] = a_grp
             if c == 0:
-                sums_ps = ps_out.tile([K, D + 1], F32, tag="sums")
+                sums_ps = ps_out.tile([K, D + P], F32, tag="sums")
                 live[("sums", g)] = sums_ps
             for j in range(PACK):
                 nc.tensor.matmul(
-                    live[("sums", g)][:, D : D + 1],
-                    lhsT=e[:, j, :],
-                    rhs=rinv[:, j : j + 1],
+                    live[("sums", g)][:, D : D + P],
+                    lhsT=a[:, j, :],
+                    rhs=ident_f[:],
+                    is_transpose=True,
                     start=(c == 0 and j == 0),
                     stop=(c == HALVES - 1 and j == PACK - 1),
                 )
-            a_grp = work.tile([P, K, PACK], BF16, align_bytes=64)
-            nc.vector.tensor_tensor(
-                out=a_grp[:],
-                in0=e[:].rearrange("p j k -> p k j"),
-                in1=rinv[:].unsqueeze(1).to_broadcast([P, K, PACK]),
-                op=ALU.mult,
-            )
-            live[("a_grp", h)] = a_grp
 
         def regroup_x(h):
             x_grp = keep.tile([P, D, PACK], BF16, align_bytes=64)
@@ -191,12 +201,12 @@ def tile_att_patch_net_pa_s_kernel(tc, x_pat, codewords, scale, out):
                 )
 
         def residual(g):
-            neg_asum = keep.tile([K, 1], F32)
-            nc.vector.tensor_scalar_mul(out=neg_asum[:], in0=live[("sums", g)][:, D : D + 1], scalar1=-1.0)
+            asum = keep.tile([K, 1], F32)
+            nc.vector.tensor_reduce(out=asum[:], in_=live[("sums", g)][:, D : D + P], axis=AX.X, op=ALU.add)
             nc.vector.scalar_tensor_tensor(
                 out=resid[:, g, :],
-                in0=cw[:],
-                scalar=neg_asum[:, 0:1],
+                in0=neg_cw[:],
+                scalar=asum[:, 0:1],
                 in1=live[("sums", g)][:, 0:D],
                 op0=ALU.mult,
                 op1=ALU.add,
@@ -209,7 +219,7 @@ def tile_att_patch_net_pa_s_kernel(tc, x_pat, codewords, scale, out):
         def unit(h):
             return 0 <= h < n_units
 
-        for r in range(n_units + 5):
+        for r in range(n_units + 6):
             if unit(r):
                 transposes(r)
             if unit(r - 1):
@@ -218,19 +228,22 @@ def tile_att_patch_net_pa_s_kernel(tc, x_pat, codewords, scale, out):
                 distances(r - 2)
                 exps(r - 2)
             if unit(r - 3):
+                reciprocals(r - 3)
                 normalise(r - 3)
+            if unit(r - 4):
+                round_a(r - 4)
             if unit(r - 2):
                 quantise("x", r - 2)
             if unit(r):
                 regroup_x(r)
-            if unit(r - 5) and (r - 5) % HALVES == HALVES - 1:
-                residual((r - 5) // HALVES)
-            if unit(r - 3):
-                quantise("a", r - 3)
-            if unit(r - 3) and (r - 3) % HALVES == HALVES - 1:
-                aggregate((r - 3) // HALVES)
-            if unit(r - 5) and (r - 5) % HALVES == HALVES - 1:
-                residual_norm((r - 5) // HALVES)
+            if unit(r - 6) and (r - 6) % HALVES == HALVES - 1:
+                residual((r - 6) // HALVES)
+            if unit(r - 4):
+                quantise("a", r - 4)
+            if unit(r - 4) and (r - 4) % HALVES == HALVES - 1:
+                aggregate((r - 4) // HALVES)
+            if unit(r - 6) and (r - 6) % HALVES == HALVES - 1:
+                residual_norm((r - 6) // HALVES)
             if r - 2 == n_units - 1:
                 warm = consts.tile([P, 1], F32)
                 nc.scalar.activation(out=warm[:], in_=ones_f[:, 0:1], func=ACT.Sqrt)

@@ -32,6 +32,7 @@ def tile_att_patch_net_pa_s_kernel(tc, x_pat, codewords, scale, out):
         consts = ctx.enter_context(tc.tile_pool(name="consts", bufs=1))
         work = ctx.enter_context(tc.tile_pool(name="work", bufs=3))
         keep = ctx.enter_context(tc.tile_pool(name="keep", bufs=4))
+        packed = ctx.enter_context(tc.tile_pool(name="packed", bufs=8))
         ps_t = ctx.enter_context(tc.psum_pool(name="ps_t", bufs=2))
         ps_u = ctx.enter_context(tc.psum_pool(name="ps_u", bufs=4))
         ps_out = ctx.enter_context(tc.psum_pool(name="ps_out", bufs=2))
@@ -83,20 +84,24 @@ def tile_att_patch_net_pa_s_kernel(tc, x_pat, codewords, scale, out):
 
         live = {}
 
-        def transposes(h):
-            raw = raws[h]
+        def square_sums(h):
             x2 = keep.tile([P, PACK], F32)
             sq_junk = work.tile([P, PACK, D], BF16)
             for j in range(PACK):
                 nc.scalar.activation(
-                    out=sq_junk[:, j, :], in_=raw[:, j, :], func=ACT.Square, accum_out=x2[:, j : j + 1]
+                    out=sq_junk[:, j, :], in_=raws[h][:, j, :], func=ACT.Square, accum_out=x2[:, j : j + 1]
                 )
+            live[("x2", h)] = x2
+
+        def transposes(h):
             xT_ps = ps_t.tile([D, PACK, P], BF16)
             for j in range(PACK):
-                nc.tensor.transpose(xT_ps[:, j, :], raw[:, j, :], ident[:])
+                nc.tensor.transpose(xT_ps[:, j, :], raws[h][:, j, :], ident[:])
+            live[("xT_ps", h)] = xT_ps
+
+        def copy_transposed(h):
             xT = work.tile([D, PACK, P], BF16)
-            nc.scalar.copy(out=xT[:], in_=xT_ps[:])
-            live[("x2", h)] = x2
+            nc.vector.tensor_copy(out=xT[:], in_=live[("xT_ps", h)][:])
             live[("xT", h)] = xT
 
         def products(h):
@@ -152,19 +157,27 @@ def tile_att_patch_net_pa_s_kernel(tc, x_pat, codewords, scale, out):
                 )
             live[("a", h)] = a
 
-        def round_a(h):
-            g, c = divmod(h, HALVES)
-            a = live[("a", h)]
+        def regroup_a(h):
             a_grp = work.tile([P, K, PACK], BF16, align_bytes=64)
-            nc.vector.tensor_copy(out=a_grp[:], in_=a[:].rearrange("p j k -> p k j"))
+            nc.gpsimd.tensor_scalar(
+                out=a_grp[:],
+                in0=live[("a", h)][:].rearrange("p j k -> p k j"),
+                scalar1=1.0,
+                scalar2=0.0,
+                op0=ALU.mult,
+                op1=ALU.add,
+            )
             live[("a_grp", h)] = a_grp
+
+        def column_sums(h):
+            g, c = divmod(h, HALVES)
             if c == 0:
                 sums_ps = ps_out.tile([K, D + P], F32, tag="sums")
                 live[("sums", g)] = sums_ps
             for j in range(PACK):
                 nc.tensor.matmul(
                     live[("sums", g)][:, D : D + P],
-                    lhsT=a[:, j, :],
+                    lhsT=live[("a", h)][:, j, :],
                     rhs=ident_f[:],
                     is_transpose=True,
                     start=(c == 0 and j == 0),
@@ -173,12 +186,14 @@ def tile_att_patch_net_pa_s_kernel(tc, x_pat, codewords, scale, out):
 
         def regroup_x(h):
             x_grp = keep.tile([P, D, PACK], BF16, align_bytes=64)
-            nc.vector.tensor_copy(out=x_grp[:], in_=raws[h][:].rearrange("p j d -> p d j"))
+            nc.gpsimd.tensor_scalar(
+                out=x_grp[:], in0=raws[h][:].rearrange("p j d -> p d j"), scalar1=1.0, scalar2=0.0, op0=ALU.mult, op1=ALU.add
+            )
             live[("x_grp", h)] = x_grp
 
         def quantise(name, h):
-            codes = keep.tile([P, D], U32, align_bytes=64, tag=name + "_codes")
-            scales = keep.tile([P, D], U8, align_bytes=64, tag=name + "_scales")
+            codes = packed.tile([P, D], U32, align_bytes=64, tag=name + "_codes")
+            scales = packed.tile([P, D], U8, align_bytes=64, tag=name + "_scales")
             nc.vector.quantize_mx(
                 out=codes[:].bitcast(FP8X4),
                 scales=scales[:],
@@ -186,6 +201,12 @@ def tile_att_patch_net_pa_s_kernel(tc, x_pat, codewords, scale, out):
             )
             live[(name + "_codes", h)] = codes
             live[(name + "_scales", h)] = scales
+
+        def quantise_x(h):
+            quantise("x", h)
+
+        def quantise_a(h):
+            quantise("a", h)
 
         def aggregate(g):
             for c in range(HALVES):
@@ -216,35 +237,32 @@ def tile_att_patch_net_pa_s_kernel(tc, x_pat, codewords, scale, out):
             e_junk = work.tile([K, D], F32)
             nc.scalar.activation(out=e_junk[:], in_=resid[:, g, :], func=ACT.Square, accum_out=ssq[:, g : g + 1])
 
-        def unit(h):
-            return 0 <= h < n_units
+        def run(stage, h):
+            if 0 <= h < n_units:
+                stage(h)
 
-        for r in range(n_units + 6):
-            if unit(r):
-                transposes(r)
-            if unit(r - 1):
-                products(r - 1)
-            if unit(r - 2):
-                distances(r - 2)
-                exps(r - 2)
-            if unit(r - 3):
-                reciprocals(r - 3)
-                normalise(r - 3)
-            if unit(r - 4):
-                round_a(r - 4)
-            if unit(r - 2):
-                quantise("x", r - 2)
-            if unit(r):
-                regroup_x(r)
-            if unit(r - 6) and (r - 6) % HALVES == HALVES - 1:
-                residual((r - 6) // HALVES)
-            if unit(r - 4):
-                quantise("a", r - 4)
-            if unit(r - 4) and (r - 4) % HALVES == HALVES - 1:
-                aggregate((r - 4) // HALVES)
-            if unit(r - 6) and (r - 6) % HALVES == HALVES - 1:
-                residual_norm((r - 6) // HALVES)
-            if r - 2 == n_units - 1:
+        def run_patch(stage, h):
+            if 0 <= h < n_units and h % HALVES == HALVES - 1:
+                stage(h // HALVES)
+
+        for r in range(n_units + 8):
+            run_patch(aggregate, r - 6)
+            run(transposes, r)
+            run(products, r - 1)
+            run(column_sums, r - 5)
+            run(regroup_a, r - 5)
+            run(regroup_x, r)
+            run(square_sums, r)
+            run(exps, r - 3)
+            run(reciprocals, r - 4)
+            run(normalise, r - 4)
+            run(distances, r - 2)
+            run(copy_transposed, r)
+            run(quantise_x, r - 2)
+            run_patch(residual, r - 7)
+            run(quantise_a, r - 5)
+            run_patch(residual_norm, r - 7)
+            if r - 3 == n_units - 1:
                 warm = consts.tile([P, 1], F32)
                 nc.scalar.activation(out=warm[:], in_=ones_f[:, 0:1], func=ACT.Sqrt)
 

@@ -159,14 +159,7 @@ def tile_att_patch_net_pa_s_kernel(tc, x_pat, codewords, scale, out):
 
         def regroup_a(h):
             a_grp = work.tile([P, K, PACK], BF16, align_bytes=64)
-            nc.gpsimd.tensor_scalar(
-                out=a_grp[:],
-                in0=live[("a", h)][:].rearrange("p j k -> p k j"),
-                scalar1=1.0,
-                scalar2=0.0,
-                op0=ALU.mult,
-                op1=ALU.add,
-            )
+            nc.vector.tensor_copy(out=a_grp[:], in_=live[("a", h)][:].rearrange("p j k -> p k j"))
             live[("a_grp", h)] = a_grp
 
         def column_sums(h):
@@ -250,17 +243,17 @@ def tile_att_patch_net_pa_s_kernel(tc, x_pat, codewords, scale, out):
             run(transposes, r)
             run(products, r - 1)
             run(column_sums, r - 5)
-            run(regroup_a, r - 5)
             run(regroup_x, r)
             run(square_sums, r)
             run(exps, r - 3)
+            run(regroup_a, r - 5)
             run(reciprocals, r - 4)
             run(normalise, r - 4)
+            run(quantise_x, r - 2)
+            run(quantise_a, r - 5)
             run(distances, r - 2)
             run(copy_transposed, r)
-            run(quantise_x, r - 2)
             run_patch(residual, r - 7)
-            run(quantise_a, r - 5)
             run_patch(residual_norm, r - 7)
             if r - 3 == n_units - 1:
                 warm = consts.tile([P, 1], F32)

@@ -20,6 +20,7 @@ PIXELS = 1024
 D = 128
 K = 128
 HALVES = PIXELS // (P * PACK)
+NORM_S = 2
 
 FLOPS = 2 * 2 * IMAGES * PATCHES * PIXELS * K * D
 
@@ -32,7 +33,8 @@ def tile_att_patch_net_pa_s_kernel(tc, x_pat, codewords, scale, out):
         consts = ctx.enter_context(tc.tile_pool(name="consts", bufs=1))
         work = ctx.enter_context(tc.tile_pool(name="work", bufs=3))
         keep = ctx.enter_context(tc.tile_pool(name="keep", bufs=4))
-        packed = ctx.enter_context(tc.tile_pool(name="packed", bufs=8))
+        packed = ctx.enter_context(tc.tile_pool(name="packed", bufs=6))
+        group = ctx.enter_context(tc.tile_pool(name="group", bufs=4))
         ps_t = ctx.enter_context(tc.psum_pool(name="ps_t", bufs=2))
         ps_u = ctx.enter_context(tc.psum_pool(name="ps_u", bufs=4))
         ps_out = ctx.enter_context(tc.psum_pool(name="ps_out", bufs=2))
@@ -101,7 +103,7 @@ def tile_att_patch_net_pa_s_kernel(tc, x_pat, codewords, scale, out):
 
         def copy_transposed(h):
             xT = work.tile([D, PACK, P], BF16)
-            nc.vector.tensor_copy(out=xT[:], in_=live[("xT_ps", h)][:])
+            nc.scalar.copy(out=xT[:], in_=live[("xT_ps", h)][:])
             live[("xT", h)] = xT
 
         def products(h):
@@ -124,9 +126,11 @@ def tile_att_patch_net_pa_s_kernel(tc, x_pat, codewords, scale, out):
                     op0=ALU.add,
                     op1=ALU.mult,
                 )
-            low = keep.tile([P, PACK], F32)
-            nc.vector.tensor_reduce(out=low[:], in_=neg_z[:], axis=AX.X, op=ALU.min)
             live[("neg_z", h)] = neg_z
+
+        def minima(h):
+            low = keep.tile([P, PACK], F32)
+            nc.vector.tensor_reduce(out=low[:], in_=live[("neg_z", h)][:], axis=AX.X, op=ALU.min)
             live[("low", h)] = low
 
         def exps(h):
@@ -149,18 +153,22 @@ def tile_att_patch_net_pa_s_kernel(tc, x_pat, codewords, scale, out):
             nc.vector.reciprocal(out=rinv[:], in_=live[("esum", h)][:])
             live[("rinv", h)] = rinv
 
-        def normalise(h):
+        def normalise_s(h):
             a = work.tile([P, PACK, K], F32)
-            for j in range(PACK):
+            for j in range(NORM_S):
                 nc.scalar.activation(
                     out=a[:, j, :], in_=live[("e", h)][:, j, :], func=ACT.Copy, scale=live[("rinv", h)][:, j : j + 1]
                 )
             live[("a", h)] = a
 
+        def normalise_v(h):
+            for j in range(NORM_S, PACK):
+                nc.vector.tensor_scalar_mul(
+                    out=live[("a", h)][:, j, :], in0=live[("e", h)][:, j, :], scalar1=live[("rinv", h)][:, j : j + 1]
+                )
+
         def regroup_a(h):
-            a_grp = work.tile([P, K, PACK], BF16, align_bytes=64)
-            nc.vector.tensor_copy(out=a_grp[:], in_=live[("a", h)][:].rearrange("p j k -> p k j"))
-            live[("a_grp", h)] = a_grp
+            nc.vector.tensor_copy(out=live[("grp", h)][:, 0, :, :], in_=live[("a", h)][:].rearrange("p j k -> p k j"))
 
         def column_sums(h):
             g, c = divmod(h, HALVES)
@@ -178,38 +186,37 @@ def tile_att_patch_net_pa_s_kernel(tc, x_pat, codewords, scale, out):
                 )
 
         def regroup_x(h):
-            x_grp = keep.tile([P, D, PACK], BF16, align_bytes=64)
+            grp = group.tile([P, 2, D, PACK], BF16, align_bytes=64)
             nc.gpsimd.tensor_scalar(
-                out=x_grp[:], in0=raws[h][:].rearrange("p j d -> p d j"), scalar1=1.0, scalar2=0.0, op0=ALU.mult, op1=ALU.add
+                out=grp[:, 1, :, :],
+                in0=raws[h][:].rearrange("p j d -> p d j"),
+                scalar1=1.0,
+                scalar2=0.0,
+                op0=ALU.mult,
+                op1=ALU.add,
             )
-            live[("x_grp", h)] = x_grp
+            live[("grp", h)] = grp
 
-        def quantise(name, h):
-            codes = packed.tile([P, D], U32, align_bytes=64, tag=name + "_codes")
-            scales = packed.tile([P, D], U8, align_bytes=64, tag=name + "_scales")
+        def quantise(h):
+            codes = packed.tile([P, 2 * D], U32, align_bytes=64)
+            scales = packed.tile([P, 2 * D], U8, align_bytes=64)
             nc.vector.quantize_mx(
                 out=codes[:].bitcast(FP8X4),
                 scales=scales[:],
-                in_=live[(name + "_grp", h)][:].rearrange("p w j -> p (w j)"),
+                in_=live[("grp", h)][:].rearrange("p o w j -> p (o w j)"),
             )
-            live[(name + "_codes", h)] = codes
-            live[(name + "_scales", h)] = scales
-
-        def quantise_x(h):
-            quantise("x", h)
-
-        def quantise_a(h):
-            quantise("a", h)
+            live[("codes", h)] = codes
+            live[("scales", h)] = scales
 
         def aggregate(g):
             for c in range(HALVES):
                 h = g * HALVES + c
                 nc.tensor.matmul_mx(
                     out=live[("sums", g)][:, 0:D],
-                    lhsT=live[("a_codes", h)][:].bitcast(FP8X4),
-                    lhsT_scale=live[("a_scales", h)][:],
-                    rhs=live[("x_codes", h)][:].bitcast(FP8X4),
-                    rhs_scale=live[("x_scales", h)][:],
+                    lhsT=live[("codes", h)][:, 0:K].bitcast(FP8X4),
+                    lhsT_scale=live[("scales", h)][:, 0:K],
+                    rhs=live[("codes", h)][:, K : K + D].bitcast(FP8X4),
+                    rhs_scale=live[("scales", h)][:, K : K + D],
                     start=(c == 0),
                     stop=(c == HALVES - 1),
                 )
@@ -238,24 +245,25 @@ def tile_att_patch_net_pa_s_kernel(tc, x_pat, codewords, scale, out):
             if 0 <= h < n_units and h % HALVES == HALVES - 1:
                 stage(h // HALVES)
 
-        for r in range(n_units + 8):
+        for r in range(-1, n_units + 6):
             run_patch(aggregate, r - 6)
-            run(transposes, r)
-            run(products, r - 1)
-            run(column_sums, r - 5)
-            run(regroup_x, r)
-            run(square_sums, r)
-            run(exps, r - 3)
-            run(regroup_a, r - 5)
-            run(reciprocals, r - 4)
-            run(normalise, r - 4)
-            run(quantise_x, r - 2)
-            run(quantise_a, r - 5)
-            run(distances, r - 2)
+            run(regroup_x, r - 2)
             run(copy_transposed, r)
-            run_patch(residual, r - 7)
-            run_patch(residual_norm, r - 7)
-            if r - 3 == n_units - 1:
+            run(products, r)
+            run(transposes, r + 1)
+            run(column_sums, r - 4)
+            run(square_sums, r + 1)
+            run(reciprocals, r - 3)
+            run(exps, r - 2)
+            run(distances, r - 1)
+            run_patch(residual, r - 6)
+            run(normalise_s, r - 3)
+            run(minima, r - 1)
+            run(normalise_v, r - 3)
+            run(quantise, r - 5)
+            run(regroup_a, r - 4)
+            run_patch(residual_norm, r - 6)
+            if r - 2 == n_units - 1:
                 warm = consts.tile([P, 1], F32)
                 nc.scalar.activation(out=warm[:], in_=ones_f[:, 0:1], func=ACT.Sqrt)
 

@@ -20,6 +20,7 @@ PIXELS = 1024
 D = 128
 K = 128
 HALVES = PIXELS // (P * PACK)
+BANK = 512
 NORM_S = 2
 
 FLOPS = 2 * 2 * IMAGES * PATCHES * PIXELS * K * D
@@ -36,7 +37,7 @@ def tile_att_patch_net_pa_s_kernel(tc, x_pat, codewords, scale, out):
         packed = ctx.enter_context(tc.tile_pool(name="packed", bufs=6))
         group = ctx.enter_context(tc.tile_pool(name="group", bufs=4))
         ps_t = ctx.enter_context(tc.psum_pool(name="ps_t", bufs=2))
-        ps_u = ctx.enter_context(tc.psum_pool(name="ps_u", bufs=4))
+        ps_u = ctx.enter_context(tc.psum_pool(name="ps_u", bufs=1))
         ps_out = ctx.enter_context(tc.psum_pool(name="ps_out", bufs=2))
         ctx.enter_context(tc.manual_schedule())
 
@@ -73,10 +74,10 @@ def tile_att_patch_net_pa_s_kernel(tc, x_pat, codewords, scale, out):
         c2_rows = consts.tile([K, P], F32)
         nc.vector.tensor_copy(out=c2_rows[:], in_=c2[:, 0:1].to_broadcast([K, P]))
 
-        s_ps = ps_u.tile([P, K], F32, tag="u_ps")
-        nc.tensor.matmul(s_ps[:], lhsT=ones_bf[:], rhs=s_rows[:], start=True, stop=True)
+        s_ps = ps_u.tile([P, BANK], F32, name="u_ps0")
+        nc.tensor.matmul(s_ps[:, 0:K], lhsT=ones_bf[:], rhs=s_rows[:], start=True, stop=True)
         neg_s_all = consts.tile([P, K], F32)
-        nc.vector.tensor_scalar_mul(out=neg_s_all[:], in0=s_ps[:], scalar1=-1.0)
+        nc.vector.tensor_scalar_mul(out=neg_s_all[:], in0=s_ps[:, 0:K], scalar1=-1.0)
 
         neg_cw = consts.tile([K, D], BF16)
         nc.vector.tensor_scalar_mul(out=neg_cw[:], in0=cw[:], scalar1=-1.0)
@@ -96,31 +97,39 @@ def tile_att_patch_net_pa_s_kernel(tc, x_pat, codewords, scale, out):
             live[("x2", h)] = x2
 
         def transposes(h):
-            xT_ps = ps_t.tile([D, PACK, P], BF16)
+            xT_ps = ps_t.tile([D, 2 * PACK, P], BF16)
             for j in range(PACK):
                 nc.tensor.transpose(xT_ps[:, j, :], raws[h][:, j, :], ident[:])
             live[("xT_ps", h)] = xT_ps
 
         def copy_transposed(h):
             xT = work.tile([D, PACK, P], BF16)
-            nc.scalar.copy(out=xT[:], in_=live[("xT_ps", h)][:])
+            nc.scalar.copy(out=xT[:], in_=live[("xT_ps", h)][:, 0:PACK, :])
             live[("xT", h)] = xT
 
         def products(h):
-            u_ps = ps_u.tile([P, PACK, K], F32)
             for j in range(PACK):
-                nc.tensor.matmul(u_ps[:, j, :], lhsT=live[("xT", h)][:, j, :], rhs=cwT_m2[:], start=True, stop=False)
+                u_ps = ps_u.tile([P, BANK], F32, name="u_ps%d" % j)
+                nc.tensor.matmul(u_ps[:, 0:K], lhsT=live[("xT", h)][:, j, :], rhs=cwT_m2[:], start=True, stop=False)
+                live[("u", h, j)] = u_ps
+
+        def offsets(h):
+            for j in range(PACK):
                 nc.tensor.matmul(
-                    u_ps[:, j, :], lhsT=c2_rows[:], rhs=ident_f[:], is_transpose=True, start=False, stop=True
+                    live[("u", h, j)][:, 0:K],
+                    lhsT=c2_rows[:],
+                    rhs=ident_f[:],
+                    is_transpose=True,
+                    start=False,
+                    stop=True,
                 )
-            live[("u", h)] = u_ps
 
         def distances(h):
             neg_z = work.tile([P, PACK, K], F32)
             for j in range(PACK):
                 nc.vector.scalar_tensor_tensor(
                     out=neg_z[:, j, :],
-                    in0=live[("u", h)][:, j, :],
+                    in0=live[("u", h, j)][:, 0:K],
                     scalar=live[("x2", h)][:, j : j + 1],
                     in1=neg_s_all[:],
                     op0=ALU.add,
@@ -173,7 +182,7 @@ def tile_att_patch_net_pa_s_kernel(tc, x_pat, codewords, scale, out):
         def column_sums(h):
             g, c = divmod(h, HALVES)
             if c == 0:
-                sums_ps = ps_out.tile([K, D + P], F32, tag="sums")
+                sums_ps = ps_out.tile([K, BANK], F32, tag="sums")
                 live[("sums", g)] = sums_ps
             for j in range(PACK):
                 nc.tensor.matmul(
@@ -246,16 +255,17 @@ def tile_att_patch_net_pa_s_kernel(tc, x_pat, codewords, scale, out):
                 stage(h // HALVES)
 
         for r in range(-1, n_units + 6):
-            run_patch(aggregate, r - 6)
+            run(column_sums, r - 4)
             run(regroup_x, r - 2)
             run(copy_transposed, r)
-            run(products, r)
             run(transposes, r + 1)
-            run(column_sums, r - 4)
+            run_patch(aggregate, r - 6)
             run(square_sums, r + 1)
             run(reciprocals, r - 3)
             run(exps, r - 2)
             run(distances, r - 1)
+            run(products, r)
+            run(offsets, r)
             run_patch(residual, r - 6)
             run(normalise_s, r - 3)
             run(minima, r - 1)

@@ -37,8 +37,8 @@ def tile_att_patch_net_pa_s_kernel(tc, x_pat, codewords, scale, out):
         packed = ctx.enter_context(tc.tile_pool(name="packed", bufs=6))
         group = ctx.enter_context(tc.tile_pool(name="group", bufs=4))
         ps_t = ctx.enter_context(tc.psum_pool(name="ps_t", bufs=2))
-        ps_u = ctx.enter_context(tc.psum_pool(name="ps_u", bufs=1))
-        ps_out = ctx.enter_context(tc.psum_pool(name="ps_out", bufs=2))
+        ps_u = ctx.enter_context(tc.psum_pool(name="ps_u", bufs=3))
+        ps_out = ctx.enter_context(tc.psum_pool(name="ps_out", bufs=3))
         ctx.enter_context(tc.manual_schedule())
 
         cw = consts.tile([K, D], BF16)
@@ -74,7 +74,7 @@ def tile_att_patch_net_pa_s_kernel(tc, x_pat, codewords, scale, out):
         c2_rows = consts.tile([K, P], F32)
         nc.vector.tensor_copy(out=c2_rows[:], in_=c2[:, 0:1].to_broadcast([K, P]))
 
-        s_ps = ps_u.tile([P, BANK], F32, name="u_ps0")
+        s_ps = ps_u.tile([P, BANK], F32, tag="u_ps")
         nc.tensor.matmul(s_ps[:, 0:K], lhsT=ones_bf[:], rhs=s_rows[:], start=True, stop=True)
         neg_s_all = consts.tile([P, K], F32)
         nc.vector.tensor_scalar_mul(out=neg_s_all[:], in0=s_ps[:, 0:K], scalar1=-1.0)
@@ -82,8 +82,9 @@ def tile_att_patch_net_pa_s_kernel(tc, x_pat, codewords, scale, out):
         neg_cw = consts.tile([K, D], BF16)
         nc.vector.tensor_scalar_mul(out=neg_cw[:], in0=cw[:], scalar1=-1.0)
 
-        resid = consts.tile([K, n_patches, D], F32)
-        ssq = consts.tile([K, n_patches], F32)
+        minus_half = consts.tile([P, 1], F32)
+        nc.vector.memset(minus_half[:], -0.5)
+        accs = [consts.tile([K, D], F32, name="acc%d" % b) for b in range(IMAGES)]
 
         live = {}
 
@@ -107,21 +108,22 @@ def tile_att_patch_net_pa_s_kernel(tc, x_pat, codewords, scale, out):
             nc.scalar.copy(out=xT[:], in_=live[("xT_ps", h)][:, 0:PACK, :])
             live[("xT", h)] = xT
 
-        def products(h):
-            for j in range(PACK):
-                u_ps = ps_u.tile([P, BANK], F32, name="u_ps%d" % j)
-                nc.tensor.matmul(u_ps[:, 0:K], lhsT=live[("xT", h)][:, j, :], rhs=cwT_m2[:], start=True, stop=False)
-                live[("u", h, j)] = u_ps
-
         def offsets(h):
+            u_ps = ps_u.tile([P, PACK, K], F32)
             for j in range(PACK):
                 nc.tensor.matmul(
-                    live[("u", h, j)][:, 0:K],
-                    lhsT=c2_rows[:],
-                    rhs=ident_f[:],
-                    is_transpose=True,
+                    u_ps[:, j, :], lhsT=c2_rows[:], rhs=ident_f[:], is_transpose=True, start=(j == 0), stop=False
+                )
+            live[("u", h)] = u_ps
+
+        def products(h):
+            for j in range(PACK):
+                nc.tensor.matmul(
+                    live[("u", h)][:, j, :],
+                    lhsT=live[("xT", h)][:, j, :],
+                    rhs=cwT_m2[:],
                     start=False,
-                    stop=True,
+                    stop=(j == PACK - 1),
                 )
 
         def distances(h):
@@ -129,7 +131,7 @@ def tile_att_patch_net_pa_s_kernel(tc, x_pat, codewords, scale, out):
             for j in range(PACK):
                 nc.vector.scalar_tensor_tensor(
                     out=neg_z[:, j, :],
-                    in0=live[("u", h, j)][:, 0:K],
+                    in0=live[("u", h)][:, j, :],
                     scalar=live[("x2", h)][:, j : j + 1],
                     in1=neg_s_all[:],
                     op0=ALU.add,
@@ -230,21 +232,61 @@ def tile_att_patch_net_pa_s_kernel(tc, x_pat, codewords, scale, out):
                     stop=(c == HALVES - 1),
                 )
 
-        def residual(g):
+        def a_sums(g):
             asum = keep.tile([K, 1], F32)
             nc.vector.tensor_reduce(out=asum[:], in_=live[("sums", g)][:, D : D + P], axis=AX.X, op=ALU.add)
+            live[("asum", g)] = asum
+
+        def residual(g):
+            resid = keep.tile([K, D], F32)
             nc.vector.scalar_tensor_tensor(
-                out=resid[:, g, :],
+                out=resid[:],
                 in0=neg_cw[:],
-                scalar=asum[:, 0:1],
+                scalar=live[("asum", g)][:, 0:1],
                 in1=live[("sums", g)][:, 0:D],
                 op0=ALU.mult,
                 op1=ALU.add,
             )
+            live[("resid", g)] = resid
 
-        def residual_norm(g):
+        def residual_squares(g):
             e_junk = work.tile([K, D], F32)
-            nc.scalar.activation(out=e_junk[:], in_=resid[:, g, :], func=ACT.Square, accum_out=ssq[:, g : g + 1])
+            ssq = keep.tile([K, 1], F32)
+            nc.scalar.activation(out=e_junk[:], in_=live[("resid", g)][:], func=ACT.Square, accum_out=ssq[:])
+            live[("ssq", g)] = ssq
+
+        def total_squares(g):
+            nc.tensor.matmul(
+                live[("sums", g)][:, D : D + 1], lhsT=ones_f[:], rhs=live[("ssq", g)][:], start=True, stop=True
+            )
+
+        def floor_totals(g):
+            total = keep.tile([P, 1], F32)
+            nc.vector.tensor_scalar_max(out=total[:], in0=live[("sums", g)][:, D : D + 1], scalar1=1e-24)
+            live[("total", g)] = total
+
+        def norm_reciprocals(g):
+            rnorm = keep.tile([P, 1], F32)
+            nc.gpsimd.tensor_tensor(out=rnorm[:], in0=live[("total", g)][:], in1=minus_half[:], op=ALU.pow)
+            live[("rnorm", g)] = rnorm
+
+        def accumulate(g):
+            b, t = divmod(g, PATCHES)
+            if t == 0:
+                nc.vector.tensor_scalar_mul(
+                    out=accs[b][:], in0=live[("resid", g)][:], scalar1=live[("rnorm", g)][:, 0:1]
+                )
+            else:
+                nc.vector.scalar_tensor_tensor(
+                    out=accs[b][:],
+                    in0=live[("resid", g)][:],
+                    scalar=live[("rnorm", g)][:, 0:1],
+                    in1=accs[b][:],
+                    op0=ALU.mult,
+                    op1=ALU.add,
+                )
+            if t == PATCHES - 1:
+                nc.sync.dma_start(out=out[b].rearrange("(k d) -> k d", d=D), in_=accs[b][:])
 
         def run(stage, h):
             if 0 <= h < n_units:
@@ -254,50 +296,27 @@ def tile_att_patch_net_pa_s_kernel(tc, x_pat, codewords, scale, out):
             if 0 <= h < n_units and h % HALVES == HALVES - 1:
                 stage(h // HALVES)
 
-        for r in range(-1, n_units + 6):
-            run(column_sums, r - 4)
-            run(regroup_x, r - 2)
+        for r in range(-1, n_units + 8):
             run(copy_transposed, r)
-            run(transposes, r + 1)
-            run_patch(aggregate, r - 6)
-            run(square_sums, r + 1)
             run(reciprocals, r - 3)
             run(exps, r - 2)
             run(distances, r - 1)
+            run(column_sums, r - 4)
+            run(transposes, r + 1)
+            run(offsets, r + 1)
+            run_patch(aggregate, r - 6)
             run(products, r)
-            run(offsets, r)
-            run_patch(residual, r - 6)
+            run_patch(total_squares, r - 7)
+            run(regroup_x, r - 2)
             run(normalise_s, r - 3)
-            run(minima, r - 1)
-            run(normalise_v, r - 3)
-            run(quantise, r - 5)
+            run(square_sums, r + 1)
+            run_patch(a_sums, r - 6)
             run(regroup_a, r - 4)
-            run_patch(residual_norm, r - 6)
-            if r - 2 == n_units - 1:
-                warm = consts.tile([P, 1], F32)
-                nc.scalar.activation(out=warm[:], in_=ones_f[:, 0:1], func=ACT.Sqrt)
-
-        tot_ps = ps_out.tile([P, n_patches], F32, tag="sums")
-        nc.tensor.matmul(tot_ps[:], lhsT=ones_f[:], rhs=ssq[:], start=True, stop=True)
-        norm = keep.tile([P, n_patches], F32)
-        nc.scalar.activation(out=norm[:], in_=tot_ps[:], func=ACT.Sqrt)
-        nc.vector.tensor_scalar_max(out=norm[:], in0=norm[:], scalar1=1e-12)
-        rnorm = keep.tile([P, n_patches], F32)
-        nc.vector.reciprocal(out=rnorm[:], in_=norm[:])
-        accs = [consts.tile([K, D], F32, name="acc%d" % b) for b in range(IMAGES)]
-        for t in range(PATCHES):
-            for b in range(IMAGES):
-                g = b * PATCHES + t
-                if t == 0:
-                    nc.vector.tensor_scalar_mul(out=accs[b][:], in0=resid[:, g, :], scalar1=rnorm[:, g : g + 1])
-                else:
-                    nc.vector.scalar_tensor_tensor(
-                        out=accs[b][:],
-                        in0=resid[:, g, :],
-                        scalar=rnorm[:, g : g + 1],
-                        in1=accs[b][:],
-                        op0=ALU.mult,
-                        op1=ALU.add,
-                    )
-        nc.sync.dma_start(out=out[0].rearrange("(k d) -> k d", d=D), in_=accs[0][:])
-        nc.scalar.dma_start(out=out[1].rearrange("(k d) -> k d", d=D), in_=accs[1][:])
+            run(minima, r - 1)
+            run_patch(residual, r - 6)
+            run(normalise_v, r - 3)
+            run_patch(accumulate, r - 8)
+            run_patch(floor_totals, r - 7)
+            run_patch(norm_reciprocals, r - 7)
+            run(quantise, r - 5)
+            run_patch(residual_squares, r - 6)

@@ -82,8 +82,8 @@ def tile_att_patch_net_pa_s_kernel(tc, x_pat, codewords, scale, out):
         neg_cw = consts.tile([K, D], BF16)
         nc.vector.tensor_scalar_mul(out=neg_cw[:], in0=cw[:], scalar1=-1.0)
 
-        minus_half = consts.tile([P, 1], F32)
-        nc.vector.memset(minus_half[:], -0.5)
+        resid = consts.tile([K, n_patches, D], F32)
+        ssq = consts.tile([K, n_patches], F32)
         accs = [consts.tile([K, D], F32, name="acc%d" % b) for b in range(IMAGES)]
 
         live = {}
@@ -238,49 +238,41 @@ def tile_att_patch_net_pa_s_kernel(tc, x_pat, codewords, scale, out):
             live[("asum", g)] = asum
 
         def residual(g):
-            resid = keep.tile([K, D], F32)
             nc.vector.scalar_tensor_tensor(
-                out=resid[:],
+                out=resid[:, g, :],
                 in0=neg_cw[:],
                 scalar=live[("asum", g)][:, 0:1],
                 in1=live[("sums", g)][:, 0:D],
                 op0=ALU.mult,
                 op1=ALU.add,
             )
-            live[("resid", g)] = resid
 
         def residual_squares(g):
             e_junk = work.tile([K, D], F32)
-            ssq = keep.tile([K, 1], F32)
-            nc.scalar.activation(out=e_junk[:], in_=live[("resid", g)][:], func=ACT.Square, accum_out=ssq[:])
-            live[("ssq", g)] = ssq
+            nc.scalar.activation(out=e_junk[:], in_=resid[:, g, :], func=ACT.Square, accum_out=ssq[:, g : g + 1])
 
-        def total_squares(g):
-            nc.tensor.matmul(
-                live[("sums", g)][:, D : D + 1], lhsT=ones_f[:], rhs=live[("ssq", g)][:], start=True, stop=True
-            )
-
-        def floor_totals(g):
-            total = keep.tile([P, 1], F32)
-            nc.vector.tensor_scalar_max(out=total[:], in0=live[("sums", g)][:, D : D + 1], scalar1=1e-24)
-            live[("total", g)] = total
-
-        def norm_reciprocals(g):
-            rnorm = keep.tile([P, 1], F32)
-            nc.gpsimd.tensor_tensor(out=rnorm[:], in0=live[("total", g)][:], in1=minus_half[:], op=ALU.pow)
-            live[("rnorm", g)] = rnorm
+        def norms(g0, g1):
+            n = g1 - g0
+            total = ps_out.tile([K, BANK], F32, tag="sums")
+            nc.tensor.matmul(total[:, 0:n], lhsT=ones_f[:], rhs=ssq[:, g0:g1], start=True, stop=True)
+            norm = keep.tile([P, n_patches], F32)
+            nc.scalar.activation(out=norm[:, 0:n], in_=total[:, 0:n], func=ACT.Sqrt)
+            floored = keep.tile([P, n_patches], F32)
+            nc.vector.tensor_scalar_max(out=floored[:, 0:n], in0=norm[:, 0:n], scalar1=1e-12)
+            rnorm = keep.tile([P, n_patches], F32)
+            nc.vector.reciprocal(out=rnorm[:, 0:n], in_=floored[:, 0:n])
+            for g in range(g0, g1):
+                live[("rnorm", g)] = rnorm[:, g - g0 : g - g0 + 1]
 
         def accumulate(g):
             b, t = divmod(g, PATCHES)
             if t == 0:
-                nc.vector.tensor_scalar_mul(
-                    out=accs[b][:], in0=live[("resid", g)][:], scalar1=live[("rnorm", g)][:, 0:1]
-                )
+                nc.vector.tensor_scalar_mul(out=accs[b][:], in0=resid[:, g, :], scalar1=live[("rnorm", g)])
             else:
                 nc.vector.scalar_tensor_tensor(
                     out=accs[b][:],
-                    in0=live[("resid", g)][:],
-                    scalar=live[("rnorm", g)][:, 0:1],
+                    in0=resid[:, g, :],
+                    scalar=live[("rnorm", g)],
                     in1=accs[b][:],
                     op0=ALU.mult,
                     op1=ALU.add,
@@ -296,18 +288,20 @@ def tile_att_patch_net_pa_s_kernel(tc, x_pat, codewords, scale, out):
             if 0 <= h < n_units and h % HALVES == HALVES - 1:
                 stage(h // HALVES)
 
-        for r in range(-1, n_units + 8):
+        last = n_patches - 1
+        for r in range(-1, n_units + 6):
             run(copy_transposed, r)
             run(reciprocals, r - 3)
             run(exps, r - 2)
+            if r - 2 == n_units:
+                warm = consts.tile([P, 1], F32)
+                nc.scalar.activation(out=warm[:], in_=ones_f[:, 0:1], func=ACT.Sqrt)
             run(distances, r - 1)
-            run(column_sums, r - 4)
             run(transposes, r + 1)
             run(offsets, r + 1)
             run_patch(aggregate, r - 6)
             run(products, r)
-            run_patch(total_squares, r - 7)
-            run(regroup_x, r - 2)
+            run(column_sums, r - 4)
             run(normalise_s, r - 3)
             run(square_sums, r + 1)
             run_patch(a_sums, r - 6)
@@ -315,8 +309,12 @@ def tile_att_patch_net_pa_s_kernel(tc, x_pat, codewords, scale, out):
             run(minima, r - 1)
             run_patch(residual, r - 6)
             run(normalise_v, r - 3)
-            run_patch(accumulate, r - 8)
-            run_patch(floor_totals, r - 7)
-            run_patch(norm_reciprocals, r - 7)
             run(quantise, r - 5)
+            run(regroup_x, r - 2)
             run_patch(residual_squares, r - 6)
+            if r - 6 == n_units - 2:
+                norms(0, last)
+                for g in (0, 4, 1, 5, 2, 6, 3):
+                    accumulate(g)
+        norms(last, n_patches)
+        accumulate(last)

@@ -21,6 +21,7 @@ D = 128
 K = 128
 HALVES = PIXELS // (P * PACK)
 BANK = 512
+CLOCK_HEAD = 4
 NORM_S = 2
 
 FLOPS = 2 * 2 * IMAGES * PATCHES * PIXELS * K * D
@@ -37,9 +38,16 @@ def tile_att_patch_net_pa_s_kernel(tc, x_pat, codewords, scale, out):
         packed = ctx.enter_context(tc.tile_pool(name="packed", bufs=6))
         group = ctx.enter_context(tc.tile_pool(name="group", bufs=4))
         ps_t = ctx.enter_context(tc.psum_pool(name="ps_t", bufs=2))
-        ps_u = ctx.enter_context(tc.psum_pool(name="ps_u", bufs=3))
+        ps_u = ctx.enter_context(tc.psum_pool(name="ps_u", bufs=2))
         ps_out = ctx.enter_context(tc.psum_pool(name="ps_out", bufs=3))
+        ps_clock = ctx.enter_context(tc.psum_pool(name="ps_clock", bufs=1))
         ctx.enter_context(tc.manual_schedule())
+
+        clock_ps = ps_clock.tile([P, BANK], F32)
+        ones_f = consts.tile([P, P], F32)
+        nc.vector.memset(ones_f[:], 1.0)
+        for i in range(CLOCK_HEAD):
+            nc.tensor.matmul(clock_ps[:, 0:P], lhsT=ones_f[:], rhs=ones_f[:], start=True, stop=True)
 
         cw = consts.tile([K, D], BF16)
         nc.scalar.dma_start(out=cw[:], in_=codewords)
@@ -60,8 +68,6 @@ def tile_att_patch_net_pa_s_kernel(tc, x_pat, codewords, scale, out):
         make_identity(nc, ident_f[:])
         ones_bf = consts.tile([P, P], BF16)
         nc.vector.memset(ones_bf[:], 1.0)
-        ones_f = consts.tile([P, P], F32)
-        nc.vector.memset(ones_f[:], 1.0)
 
         cwT_ps = ps_t.tile([D, K], BF16, tag="xT_ps")
         nc.tensor.transpose(cwT_ps[:], cw[:], ident[:])
@@ -85,6 +91,9 @@ def tile_att_patch_net_pa_s_kernel(tc, x_pat, codewords, scale, out):
         resid = consts.tile([K, n_patches, D], F32)
         ssq = consts.tile([K, n_patches], F32)
         accs = [consts.tile([K, D], F32, name="acc%d" % b) for b in range(IMAGES)]
+
+        x_codes = consts.tile([P, n_units * D], U32, align_bytes=64)
+        x_scales = consts.tile([P, n_units * D], U8, align_bytes=64)
 
         live = {}
 
@@ -179,7 +188,9 @@ def tile_att_patch_net_pa_s_kernel(tc, x_pat, codewords, scale, out):
                 )
 
         def regroup_a(h):
-            nc.vector.tensor_copy(out=live[("grp", h)][:, 0, :, :], in_=live[("a", h)][:].rearrange("p j k -> p k j"))
+            a_grp = group.tile([P, K, PACK], BF16, align_bytes=64)
+            nc.vector.tensor_copy(out=a_grp[:], in_=live[("a", h)][:].rearrange("p j k -> p k j"))
+            live[("a_grp", h)] = a_grp
 
         def column_sums(h):
             g, c = divmod(h, HALVES)
@@ -197,37 +208,57 @@ def tile_att_patch_net_pa_s_kernel(tc, x_pat, codewords, scale, out):
                 )
 
         def regroup_x(h):
-            grp = group.tile([P, 2, D, PACK], BF16, align_bytes=64)
+            x_grp = group.tile([P, D, PACK], BF16, align_bytes=64)
             nc.gpsimd.tensor_scalar(
-                out=grp[:, 1, :, :],
+                out=x_grp[:],
                 in0=raws[h][:].rearrange("p j d -> p d j"),
                 scalar1=1.0,
                 scalar2=0.0,
                 op0=ALU.mult,
                 op1=ALU.add,
             )
-            live[("grp", h)] = grp
+            live[("x_grp", h)] = x_grp
 
-        def quantise(h):
-            codes = packed.tile([P, 2 * D], U32, align_bytes=64)
-            scales = packed.tile([P, 2 * D], U8, align_bytes=64)
+        def quantise_x(h):
+            nc.vector.quantize_mx(
+                out=x_codes[:, h * D : (h + 1) * D].bitcast(FP8X4),
+                scales=x_scales[:, h * D : (h + 1) * D],
+                in_=live[("x_grp", h)][:].rearrange("p w j -> p (w j)"),
+            )
+
+        def quantise_a(h):
+            codes = packed.tile([P, K], U32, align_bytes=64)
+            scales = packed.tile([P, K], U8, align_bytes=64)
             nc.vector.quantize_mx(
                 out=codes[:].bitcast(FP8X4),
                 scales=scales[:],
-                in_=live[("grp", h)][:].rearrange("p o w j -> p (o w j)"),
+                in_=live[("a_grp", h)][:].rearrange("p w j -> p (w j)"),
             )
             live[("codes", h)] = codes
             live[("scales", h)] = scales
+
+        def clock_passes(h, count):
+            width = max(w for w in (D, 2 * D, 4 * D) if w <= (min(h, n_units - 1) + 1) * D)
+            for i in range(count):
+                nc.tensor.matmul_mx(
+                    out=clock_ps[:, 0:width],
+                    lhsT=x_codes[:, 0:D].bitcast(FP8X4),
+                    lhsT_scale=x_scales[:, 0:D],
+                    rhs=x_codes[:, 0:width].bitcast(FP8X4),
+                    rhs_scale=x_scales[:, 0:width],
+                    start=True,
+                    stop=True,
+                )
 
         def aggregate(g):
             for c in range(HALVES):
                 h = g * HALVES + c
                 nc.tensor.matmul_mx(
                     out=live[("sums", g)][:, 0:D],
-                    lhsT=live[("codes", h)][:, 0:K].bitcast(FP8X4),
-                    lhsT_scale=live[("scales", h)][:, 0:K],
-                    rhs=live[("codes", h)][:, K : K + D].bitcast(FP8X4),
-                    rhs_scale=live[("scales", h)][:, K : K + D],
+                    lhsT=live[("codes", h)][:].bitcast(FP8X4),
+                    lhsT_scale=live[("scales", h)][:],
+                    rhs=x_codes[:, h * D : (h + 1) * D].bitcast(FP8X4),
+                    rhs_scale=x_scales[:, h * D : (h + 1) * D],
                     start=(c == 0),
                     stop=(c == HALVES - 1),
                 )
@@ -298,9 +329,11 @@ def tile_att_patch_net_pa_s_kernel(tc, x_pat, codewords, scale, out):
                 nc.scalar.activation(out=warm[:], in_=ones_f[:, 0:1], func=ACT.Sqrt)
             run(distances, r - 1)
             run(transposes, r + 1)
-            run(offsets, r + 1)
             run_patch(aggregate, r - 6)
+            if 1 <= r < n_units:
+                clock_passes(r - 1, 2 - r % 2)
             run(products, r)
+            run(offsets, r + 1)
             run(column_sums, r - 4)
             run(normalise_s, r - 3)
             run(square_sums, r + 1)
@@ -309,8 +342,9 @@ def tile_att_patch_net_pa_s_kernel(tc, x_pat, codewords, scale, out):
             run(minima, r - 1)
             run_patch(residual, r - 6)
             run(normalise_v, r - 3)
-            run(quantise, r - 5)
-            run(regroup_x, r - 2)
+            run(quantise_x, r)
+            run(quantise_a, r - 5)
+            run(regroup_x, r + 1)
             run_patch(residual_squares, r - 6)
             if r - 6 == n_units - 2:
                 norms(0, last)

@@ -22,7 +22,9 @@ K = 128
 HALVES = PIXELS // (P * PACK)
 BANK = 512
 CLOCK_HEAD = 4
-NORM_S = 2
+RAMP = 2
+NORM_S = 3
+NORM_V = 1
 
 FLOPS = 2 * 2 * IMAGES * PATCHES * PIXELS * K * D
 
@@ -114,7 +116,10 @@ def tile_att_patch_net_pa_s_kernel(tc, x_pat, codewords, scale, out):
 
         def copy_transposed(h):
             xT = work.tile([D, PACK, P], BF16)
-            nc.scalar.copy(out=xT[:], in_=live[("xT_ps", h)][:, 0:PACK, :])
+            if h < RAMP:
+                nc.vector.tensor_copy(out=xT[:], in_=live[("xT_ps", h)][:, 0:PACK, :])
+            else:
+                nc.scalar.copy(out=xT[:], in_=live[("xT_ps", h)][:, 0:PACK, :])
             live[("xT", h)] = xT
 
         def offsets(h):
@@ -136,7 +141,7 @@ def tile_att_patch_net_pa_s_kernel(tc, x_pat, codewords, scale, out):
                 )
 
         def distances(h):
-            neg_z = work.tile([P, PACK, K], F32)
+            neg_z = work.tile([P, PACK, K], F32, name="neg_z")
             for j in range(PACK):
                 nc.vector.scalar_tensor_tensor(
                     out=neg_z[:, j, :],
@@ -149,8 +154,26 @@ def tile_att_patch_net_pa_s_kernel(tc, x_pat, codewords, scale, out):
             live[("neg_z", h)] = neg_z
 
         def minima(h):
-            low = keep.tile([P, PACK], F32)
+            low = keep.tile([P, PACK], F32, name="low")
             nc.vector.tensor_reduce(out=low[:], in_=live[("neg_z", h)][:], axis=AX.X, op=ALU.min)
+            live[("low", h)] = low
+
+        def distances_and_minima(h):
+            neg_z = work.tile([P, PACK, K], F32, name="neg_z")
+            low = keep.tile([P, PACK], F32, name="low")
+            for i in range(PACK + 1):
+                if i < PACK:
+                    nc.vector.scalar_tensor_tensor(
+                        out=neg_z[:, i, :],
+                        in0=live[("u", h)][:, i, :],
+                        scalar=live[("x2", h)][:, i : i + 1],
+                        in1=neg_s_all[:],
+                        op0=ALU.add,
+                        op1=ALU.mult,
+                    )
+                if i > 0:
+                    nc.vector.tensor_reduce(out=low[:, i - 1 : i], in_=neg_z[:, i - 1, :], axis=AX.X, op=ALU.min)
+            live[("neg_z", h)] = neg_z
             live[("low", h)] = low
 
         def exps(h):
@@ -172,19 +195,32 @@ def tile_att_patch_net_pa_s_kernel(tc, x_pat, codewords, scale, out):
             rinv = keep.tile([P, PACK], F32)
             nc.vector.reciprocal(out=rinv[:], in_=live[("esum", h)][:])
             live[("rinv", h)] = rinv
+            live[("a", h)] = work.tile([P, PACK, K], F32, name="a")
 
-        def normalise_s(h):
-            a = work.tile([P, PACK, K], F32)
-            for j in range(NORM_S):
+        def normalise_s(h, n_s):
+            for j in range(n_s):
                 nc.scalar.activation(
-                    out=a[:, j, :], in_=live[("e", h)][:, j, :], func=ACT.Copy, scale=live[("rinv", h)][:, j : j + 1]
+                    out=live[("a", h)][:, j, :],
+                    in_=live[("e", h)][:, j, :],
+                    func=ACT.Copy,
+                    scale=live[("rinv", h)][:, j : j + 1],
                 )
-            live[("a", h)] = a
 
-        def normalise_v(h):
-            for j in range(NORM_S, PACK):
+        def normalise_v(h, j0, j1):
+            for j in range(j0, j1):
                 nc.vector.tensor_scalar_mul(
                     out=live[("a", h)][:, j, :], in0=live[("e", h)][:, j, :], scalar1=live[("rinv", h)][:, j : j + 1]
+                )
+
+        def normalise_g(h, j0):
+            for j in range(j0, PACK):
+                nc.gpsimd.tensor_scalar(
+                    out=live[("a", h)][:, j, :],
+                    in0=live[("e", h)][:, j, :],
+                    scalar1=live[("rinv", h)][:, j : j + 1],
+                    scalar2=0.0,
+                    op0=ALU.mult,
+                    op1=ALU.add,
                 )
 
         def regroup_a(h):
@@ -239,7 +275,7 @@ def tile_att_patch_net_pa_s_kernel(tc, x_pat, codewords, scale, out):
 
         def clock_passes(h, count):
             width = max(w for w in (D, 2 * D, 4 * D) if w <= (min(h, n_units - 1) + 1) * D)
-            for i in range(count):
+            for i in range(count * 4 * D // width):
                 nc.tensor.matmul_mx(
                     out=clock_ps[:, 0:width],
                     lhsT=x_codes[:, 0:D].bitcast(FP8X4),
@@ -282,16 +318,18 @@ def tile_att_patch_net_pa_s_kernel(tc, x_pat, codewords, scale, out):
             e_junk = work.tile([K, D], F32)
             nc.scalar.activation(out=e_junk[:], in_=resid[:, g, :], func=ACT.Square, accum_out=ssq[:, g : g + 1])
 
-        def norms(g0, g1):
+        def inverse_norms(g0, g1):
             n = g1 - g0
             total = ps_out.tile([K, BANK], F32, tag="sums")
             nc.tensor.matmul(total[:, 0:n], lhsT=ones_f[:], rhs=ssq[:, g0:g1], start=True, stop=True)
-            norm = keep.tile([P, n_patches], F32)
-            nc.scalar.activation(out=norm[:, 0:n], in_=total[:, 0:n], func=ACT.Sqrt)
-            floored = keep.tile([P, n_patches], F32)
-            nc.vector.tensor_scalar_max(out=floored[:, 0:n], in0=norm[:, 0:n], scalar1=1e-12)
+            inverse = keep.tile([P, n_patches], F32)
+            nc.scalar.activation(out=inverse[:, 0:n], in_=total[:, 0:n], func=ACT.Abs_reciprocal_sqrt)
+            live[("inverse", g0)] = inverse
+
+        def bounded(g0, g1):
+            n = g1 - g0
             rnorm = keep.tile([P, n_patches], F32)
-            nc.vector.reciprocal(out=rnorm[:, 0:n], in_=floored[:, 0:n])
+            nc.vector.tensor_scalar_min(out=rnorm[:, 0:n], in0=live[("inverse", g0)][:, 0:n], scalar1=1e12)
             for g in range(g0, g1):
                 live[("rnorm", g)] = rnorm[:, g - g0 : g - g0 + 1]
 
@@ -319,36 +357,73 @@ def tile_att_patch_net_pa_s_kernel(tc, x_pat, codewords, scale, out):
             if 0 <= h < n_units and h % HALVES == HALVES - 1:
                 stage(h // HALVES)
 
-        last = n_patches - 1
-        for r in range(-1, n_units + 6):
+        def normalise(h):
+            if 0 <= h < n_units:
+                normalise_s(h, NORM_S)
+                normalise_v(h, NORM_S, NORM_S + NORM_V)
+                normalise_g(h, NORM_S + NORM_V)
+
+        last = n_units - 1
+        for r in range(-1, n_units + 1):
             run(copy_transposed, r)
             run(reciprocals, r - 3)
             run(exps, r - 2)
-            if r - 2 == n_units:
-                warm = consts.tile([P, 1], F32)
-                nc.scalar.activation(out=warm[:], in_=ones_f[:, 0:1], func=ACT.Sqrt)
-            run(distances, r - 1)
+            if r - 1 == last:
+                distances_and_minima(last)
+            else:
+                run(distances, r - 1)
             run(transposes, r + 1)
             run_patch(aggregate, r - 6)
-            if 1 <= r < n_units:
-                clock_passes(r - 1, 2 - r % 2)
             run(products, r)
+            if 1 <= r < n_units:
+                clock_passes(r - 1, 2)
             run(offsets, r + 1)
             run(column_sums, r - 4)
-            run(normalise_s, r - 3)
-            run(square_sums, r + 1)
             run_patch(a_sums, r - 6)
             run(regroup_a, r - 4)
-            run(minima, r - 1)
+            if r - 1 != last:
+                run(minima, r - 1)
             run_patch(residual, r - 6)
-            run(normalise_v, r - 3)
+            normalise(r - 3)
+            run(square_sums, r + 1)
             run(quantise_x, r)
             run(quantise_a, r - 5)
             run(regroup_x, r + 1)
             run_patch(residual_squares, r - 6)
-            if r - 6 == n_units - 2:
-                norms(0, last)
-                for g in (0, 4, 1, 5, 2, 6, 3):
-                    accumulate(g)
-        norms(last, n_patches)
-        accumulate(last)
+        exps(last)
+        reciprocals(last - 1)
+        normalise_s(last - 1, NORM_S)
+        warm = consts.tile([P, 1], F32)
+        nc.scalar.activation(out=warm[:], in_=ones_f[:, 0:1], func=ACT.Abs_reciprocal_sqrt)
+        column_sums(last - 2)
+        aggregate(5)
+        regroup_a(last - 2)
+        normalise_v(last - 1, NORM_S, PACK)
+        column_sums(last - 1)
+        quantise_a(last - 3)
+        a_sums(5)
+        quantise_a(last - 2)
+        residual(5)
+        residual_squares(5)
+        aggregate(6)
+        reciprocals(last)
+        a_sums(6)
+        regroup_a(last - 1)
+        normalise_v(last, 0, PACK)
+        column_sums(last)
+        residual(6)
+        residual_squares(6)
+        quantise_a(last - 1)
+        regroup_a(last)
+        inverse_norms(0, 7)
+        a_sums(7)
+        quantise_a(last)
+        aggregate(7)
+        residual(7)
+        bounded(0, 7)
+        residual_squares(7)
+        inverse_norms(7, 8)
+        for g in (0, 4, 1, 5, 2, 6, 3):
+            accumulate(g)
+        bounded(7, 8)
+        accumulate(7)

@@ -22,6 +22,7 @@ K = 128
 HALVES = PIXELS // (P * PACK)
 BANK = 512
 CLOCK_HEAD = 4
+RUN = 4
 RAMP = 2
 NORM_S = 3
 NORM_V = 1
@@ -225,7 +226,10 @@ def tile_att_patch_net_pa_s_kernel(tc, x_pat, codewords, scale, out):
 
         def regroup_a(h):
             a_grp = group.tile([P, K, PACK], BF16, align_bytes=64)
-            nc.vector.tensor_copy(out=a_grp[:], in_=live[("a", h)][:].rearrange("p j k -> p k j"))
+            nc.vector.tensor_copy(
+                out=a_grp[:].rearrange("p (c i) j -> p c j i", i=RUN),
+                in_=live[("a", h)][:].rearrange("p j (c i) -> p c j i", i=RUN),
+            )
             live[("a_grp", h)] = a_grp
 
         def column_sums(h):
@@ -246,8 +250,8 @@ def tile_att_patch_net_pa_s_kernel(tc, x_pat, codewords, scale, out):
         def regroup_x(h):
             x_grp = group.tile([P, D, PACK], BF16, align_bytes=64)
             nc.gpsimd.tensor_scalar(
-                out=x_grp[:],
-                in0=raws[h][:].rearrange("p j d -> p d j"),
+                out=x_grp[:].rearrange("p (c i) j -> p c j i", i=RUN),
+                in0=raws[h][:].rearrange("p j (c i) -> p c j i", i=RUN),
                 scalar1=1.0,
                 scalar2=0.0,
                 op0=ALU.mult,
@@ -359,9 +363,9 @@ def tile_att_patch_net_pa_s_kernel(tc, x_pat, codewords, scale, out):
 
         def normalise(h):
             if 0 <= h < n_units:
-                normalise_s(h, NORM_S)
-                normalise_v(h, NORM_S, NORM_S + NORM_V)
-                normalise_g(h, NORM_S + NORM_V)
+                n_s = NORM_S - 1 + h % 2
+                normalise_s(h, n_s)
+                normalise_v(h, n_s, PACK)
 
         last = n_units - 1
         for r in range(-1, n_units + 1):

from contextlib import ExitStack

import concourse.mybir as mybir
from concourse.masks import make_identity

F32 = mybir.dt.float32
BF16 = mybir.dt.bfloat16
U32 = mybir.dt.uint32
U8 = mybir.dt.uint8
FP8X4 = mybir.dt.float8_e4m3fn_x4
ALU = mybir.AluOpType
ACT = mybir.ActivationFunctionType
AX = mybir.AxisListType

P = 128
PACK = 4
IMAGES = 2
PATCHES = 4
PIXELS = 1024
D = 128
K = 128
HALVES = PIXELS // (P * PACK)
BANK = 512
CLOCK_HEAD = 4
RUN = 4
RAMP = 2
NORM_S = 3
NORM_V = 1

FLOPS = 2 * 2 * IMAGES * PATCHES * PIXELS * K * D


def tile_att_patch_net_pa_s_kernel(tc, x_pat, codewords, scale, out):
    nc = tc.nc
    n_patches = IMAGES * PATCHES
    n_units = n_patches * HALVES
    with ExitStack() as ctx:
        consts = ctx.enter_context(tc.tile_pool(name="consts", bufs=1))
        work = ctx.enter_context(tc.tile_pool(name="work", bufs=3))
        keep = ctx.enter_context(tc.tile_pool(name="keep", bufs=4))
        packed = ctx.enter_context(tc.tile_pool(name="packed", bufs=6))
        group = ctx.enter_context(tc.tile_pool(name="group", bufs=4))
        ps_t = ctx.enter_context(tc.psum_pool(name="ps_t", bufs=2))
        ps_u = ctx.enter_context(tc.psum_pool(name="ps_u", bufs=2))
        ps_out = ctx.enter_context(tc.psum_pool(name="ps_out", bufs=3))
        ps_clock = ctx.enter_context(tc.psum_pool(name="ps_clock", bufs=1))
        ctx.enter_context(tc.manual_schedule())

        clock_ps = ps_clock.tile([P, BANK], F32)
        ones_f = consts.tile([P, P], F32)
        nc.vector.memset(ones_f[:], 1.0)
        for i in range(CLOCK_HEAD):
            nc.tensor.matmul(clock_ps[:, 0:P], lhsT=ones_f[:], rhs=ones_f[:], start=True, stop=True)

        cw = consts.tile([K, D], BF16)
        nc.scalar.dma_start(out=cw[:], in_=codewords)
        s_rows = consts.tile([P, K], BF16)
        nc.vector.memset(s_rows[:], 0.0)
        nc.scalar.dma_start(out=s_rows[0:1, :], in_=scale.unsqueeze(0))
        raws = []
        for h in range(n_units):
            g, c = divmod(h, HALVES)
            raw = consts.tile([P, PACK, D], BF16, name="raw%d" % h)
            rows = x_pat[g // PATCHES, g % PATCHES, c * P * PACK : (c + 1) * P * PACK, :]
            nc.sync.dma_start(out=raw[:], in_=rows.rearrange("(p j) d -> p j d", j=PACK))
            raws.append(raw)

        ident = consts.tile([P, P], BF16)
        make_identity(nc, ident[:])
        ident_f = consts.tile([P, P], F32)
        make_identity(nc, ident_f[:])
        ones_bf = consts.tile([P, P], BF16)
        nc.vector.memset(ones_bf[:], 1.0)

        cwT_ps = ps_t.tile([D, K], BF16, tag="xT_ps")
        nc.tensor.transpose(cwT_ps[:], cw[:], ident[:])
        cwT_m2 = consts.tile([D, K], BF16)
        nc.vector.tensor_scalar_mul(out=cwT_m2[:], in0=cwT_ps[:], scalar1=-2.0)

        c2 = consts.tile([K, 1], F32)
        cw_junk = consts.tile([K, D], F32)
        nc.scalar.activation(out=cw_junk[:], in_=cw[:], func=ACT.Square, accum_out=c2[:])
        c2_rows = consts.tile([K, P], F32)
        nc.vector.tensor_copy(out=c2_rows[:], in_=c2[:, 0:1].to_broadcast([K, P]))

        s_ps = ps_u.tile([P, BANK], F32, tag="u_ps")
        nc.tensor.matmul(s_ps[:, 0:K], lhsT=ones_bf[:], rhs=s_rows[:], start=True, stop=True)
        neg_s_all = consts.tile([P, K], F32)
        nc.vector.tensor_scalar_mul(out=neg_s_all[:], in0=s_ps[:, 0:K], scalar1=-1.0)

        neg_cw = consts.tile([K, D], BF16)
        nc.vector.tensor_scalar_mul(out=neg_cw[:], in0=cw[:], scalar1=-1.0)

        resid = consts.tile([K, n_patches, D], F32)
        ssq = consts.tile([K, n_patches], F32)
        accs = [consts.tile([K, D], F32, name="acc%d" % b) for b in range(IMAGES)]

        x_codes = consts.tile([P, n_units * D], U32, align_bytes=64)
        x_scales = consts.tile([P, n_units * D], U8, align_bytes=64)

        live = {}

        def square_sums(h):
            x2 = keep.tile([P, PACK], F32)
            sq_junk = work.tile([P, PACK, D], BF16)
            for j in range(PACK):
                nc.scalar.activation(
                    out=sq_junk[:, j, :], in_=raws[h][:, j, :], func=ACT.Square, accum_out=x2[:, j : j + 1]
                )
            live[("x2", h)] = x2

        def transposes(h):
            xT_ps = ps_t.tile([D, 2 * PACK, P], BF16)
            for j in range(PACK):
                nc.tensor.transpose(xT_ps[:, j, :], raws[h][:, j, :], ident[:])
            live[("xT_ps", h)] = xT_ps

        def copy_transposed(h):
            xT = work.tile([D, PACK, P], BF16)
            if h < RAMP:
                nc.vector.tensor_copy(out=xT[:], in_=live[("xT_ps", h)][:, 0:PACK, :])
            else:
                nc.scalar.copy(out=xT[:], in_=live[("xT_ps", h)][:, 0:PACK, :])
            live[("xT", h)] = xT

        def offsets(h):
            u_ps = ps_u.tile([P, PACK, K], F32)
            for j in range(PACK):
                nc.tensor.matmul(
                    u_ps[:, j, :], lhsT=c2_rows[:], rhs=ident_f[:], is_transpose=True, start=(j == 0), stop=False
                )
            live[("u", h)] = u_ps

        def products(h):
            for j in range(PACK):
                nc.tensor.matmul(
                    live[("u", h)][:, j, :],
                    lhsT=live[("xT", h)][:, j, :],
                    rhs=cwT_m2[:],
                    start=False,
                    stop=(j == PACK - 1),
                )

        def distances(h):
            neg_z = work.tile([P, PACK, K], F32, name="neg_z")
            for j in range(PACK):
                nc.vector.scalar_tensor_tensor(
                    out=neg_z[:, j, :],
                    in0=live[("u", h)][:, j, :],
                    scalar=live[("x2", h)][:, j : j + 1],
                    in1=neg_s_all[:],
                    op0=ALU.add,
                    op1=ALU.mult,
                )
            live[("neg_z", h)] = neg_z

        def minima(h):
            low = keep.tile([P, PACK], F32, name="low")
            nc.vector.tensor_reduce(out=low[:], in_=live[("neg_z", h)][:], axis=AX.X, op=ALU.min)
            live[("low", h)] = low

        def distances_and_minima(h):
            neg_z = work.tile([P, PACK, K], F32, name="neg_z")
            low = keep.tile([P, PACK], F32, name="low")
            for i in range(PACK + 1):
                if i < PACK:
                    nc.vector.scalar_tensor_tensor(
                        out=neg_z[:, i, :],
                        in0=live[("u", h)][:, i, :],
                        scalar=live[("x2", h)][:, i : i + 1],
                        in1=neg_s_all[:],
                        op0=ALU.add,
                        op1=ALU.mult,
                    )
                if i > 0:
                    nc.vector.tensor_reduce(out=low[:, i - 1 : i], in_=neg_z[:, i - 1, :], axis=AX.X, op=ALU.min)
            live[("neg_z", h)] = neg_z
            live[("low", h)] = low

        def exps(h):
            e = work.tile([P, PACK, K], F32)
            esum = keep.tile([P, PACK], F32)
            for j in range(PACK):
                nc.scalar.activation(
                    out=e[:, j, :],
                    in_=live[("neg_z", h)][:, j, :],
                    func=ACT.Exp,
                    bias=live[("low", h)][:, j : j + 1],
                    scale=-1.0,
                    accum_out=esum[:, j : j + 1],
                )
            live[("e", h)] = e
            live[("esum", h)] = esum

        def reciprocals(h):
            rinv = keep.tile([P, PACK], F32)
            nc.vector.reciprocal(out=rinv[:], in_=live[("esum", h)][:])
            live[("rinv", h)] = rinv
            live[("a", h)] = work.tile([P, PACK, K], F32, name="a")

        def normalise_s(h, n_s):
            for j in range(n_s):
                nc.scalar.activation(
                    out=live[("a", h)][:, j, :],
                    in_=live[("e", h)][:, j, :],
                    func=ACT.Copy,
                    scale=live[("rinv", h)][:, j : j + 1],
                )

        def normalise_v(h, j0, j1):
            for j in range(j0, j1):
                nc.vector.tensor_scalar_mul(
                    out=live[("a", h)][:, j, :], in0=live[("e", h)][:, j, :], scalar1=live[("rinv", h)][:, j : j + 1]
                )

        def normalise_g(h, j0):
            for j in range(j0, PACK):
                nc.gpsimd.tensor_scalar(
                    out=live[("a", h)][:, j, :],
                    in0=live[("e", h)][:, j, :],
                    scalar1=live[("rinv", h)][:, j : j + 1],
                    scalar2=0.0,
                    op0=ALU.mult,
                    op1=ALU.add,
                )

        def regroup_a(h):
            a_grp = group.tile([P, K, PACK], BF16, align_bytes=64)
            nc.vector.tensor_copy(
                out=a_grp[:].rearrange("p (c i) j -> p c j i", i=RUN),
                in_=live[("a", h)][:].rearrange("p j (c i) -> p c j i", i=RUN),
            )
            live[("a_grp", h)] = a_grp

        def column_sums(h):
            g, c = divmod(h, HALVES)
            if c == 0:
                sums_ps = ps_out.tile([K, BANK], F32, tag="sums")
                live[("sums", g)] = sums_ps
            for j in range(PACK):
                nc.tensor.matmul(
                    live[("sums", g)][:, D : D + P],
                    lhsT=live[("a", h)][:, j, :],
                    rhs=ident_f[:],
                    is_transpose=True,
                    start=(c == 0 and j == 0),
                    stop=(c == HALVES - 1 and j == PACK - 1),
                )

        def regroup_x(h):
            x_grp = group.tile([P, D, PACK], BF16, align_bytes=64)
            nc.gpsimd.tensor_scalar(
                out=x_grp[:].rearrange("p (c i) j -> p c j i", i=RUN),
                in0=raws[h][:].rearrange("p j (c i) -> p c j i", i=RUN),
                scalar1=1.0,
                scalar2=0.0,
                op0=ALU.mult,
                op1=ALU.add,
            )
            live[("x_grp", h)] = x_grp

        def quantise_x(h):
            nc.vector.quantize_mx(
                out=x_codes[:, h * D : (h + 1) * D].bitcast(FP8X4),
                scales=x_scales[:, h * D : (h + 1) * D],
                in_=live[("x_grp", h)][:].rearrange("p w j -> p (w j)"),
            )

        def quantise_a(h):
            codes = packed.tile([P, K], U32, align_bytes=64)
            scales = packed.tile([P, K], U8, align_bytes=64)
            nc.vector.quantize_mx(
                out=codes[:].bitcast(FP8X4),
                scales=scales[:],
                in_=live[("a_grp", h)][:].rearrange("p w j -> p (w j)"),
            )
            live[("codes", h)] = codes
            live[("scales", h)] = scales

        def clock_passes(h, count):
            width = max(w for w in (D, 2 * D, 4 * D) if w <= (min(h, n_units - 1) + 1) * D)
            for i in range(count * 4 * D // width):
                nc.tensor.matmul_mx(
                    out=clock_ps[:, 0:width],
                    lhsT=x_codes[:, 0:D].bitcast(FP8X4),
                    lhsT_scale=x_scales[:, 0:D],
                    rhs=x_codes[:, 0:width].bitcast(FP8X4),
                    rhs_scale=x_scales[:, 0:width],
                    start=True,
                    stop=True,
                )

        def aggregate(g):
            for c in range(HALVES):
                h = g * HALVES + c
                nc.tensor.matmul_mx(
                    out=live[("sums", g)][:, 0:D],
                    lhsT=live[("codes", h)][:].bitcast(FP8X4),
                    lhsT_scale=live[("scales", h)][:],
                    rhs=x_codes[:, h * D : (h + 1) * D].bitcast(FP8X4),
                    rhs_scale=x_scales[:, h * D : (h + 1) * D],
                    start=(c == 0),
                    stop=(c == HALVES - 1),
                )

        def a_sums(g):
            asum = keep.tile([K, 1], F32)
            nc.vector.tensor_reduce(out=asum[:], in_=live[("sums", g)][:, D : D + P], axis=AX.X, op=ALU.add)
            live[("asum", g)] = asum

        def residual(g):
            nc.vector.scalar_tensor_tensor(
                out=resid[:, g, :],
                in0=neg_cw[:],
                scalar=live[("asum", g)][:, 0:1],
                in1=live[("sums", g)][:, 0:D],
                op0=ALU.mult,
                op1=ALU.add,
            )

        def residual_squares(g):
            e_junk = work.tile([K, D], F32)
            nc.scalar.activation(out=e_junk[:], in_=resid[:, g, :], func=ACT.Square, accum_out=ssq[:, g : g + 1])

        def inverse_norms(g0, g1):
            n = g1 - g0
            total = ps_out.tile([K, BANK], F32, tag="sums")
            nc.tensor.matmul(total[:, 0:n], lhsT=ones_f[:], rhs=ssq[:, g0:g1], start=True, stop=True)
            inverse = keep.tile([P, n_patches], F32)
            nc.scalar.activation(out=inverse[:, 0:n], in_=total[:, 0:n], func=ACT.Abs_reciprocal_sqrt)
            live[("inverse", g0)] = inverse

        def bounded(g0, g1):
            n = g1 - g0
            rnorm = keep.tile([P, n_patches], F32)
            nc.vector.tensor_scalar_min(out=rnorm[:, 0:n], in0=live[("inverse", g0)][:, 0:n], scalar1=1e12)
            for g in range(g0, g1):
                live[("rnorm", g)] = rnorm[:, g - g0 : g - g0 + 1]

        def accumulate(g):
            b, t = divmod(g, PATCHES)
            if t == 0:
                nc.vector.tensor_scalar_mul(out=accs[b][:], in0=resid[:, g, :], scalar1=live[("rnorm", g)])
            else:
                nc.vector.scalar_tensor_tensor(
                    out=accs[b][:],
                    in0=resid[:, g, :],
                    scalar=live[("rnorm", g)],
                    in1=accs[b][:],
                    op0=ALU.mult,
                    op1=ALU.add,
                )
            if t == PATCHES - 1:
                nc.sync.dma_start(out=out[b].rearrange("(k d) -> k d", d=D), in_=accs[b][:])

        def run(stage, h):
            if 0 <= h < n_units:
                stage(h)

        def run_patch(stage, h):
            if 0 <= h < n_units and h % HALVES == HALVES - 1:
                stage(h // HALVES)

        def normalise(h):
            if 0 <= h < n_units:
                n_s = NORM_S - 1 + h % 2
                normalise_s(h, n_s)
                normalise_v(h, n_s, PACK)

        last = n_units - 1
        for r in range(-1, n_units + 1):
            run(copy_transposed, r)
            run(reciprocals, r - 3)
            run(exps, r - 2)
            if r - 1 == last:
                distances_and_minima(last)
            else:
                run(distances, r - 1)
            run(transposes, r + 1)
            run_patch(aggregate, r - 6)
            run(products, r)
            if 1 <= r < n_units:
                clock_passes(r - 1, 2)
            run(offsets, r + 1)
            run(column_sums, r - 4)
            run_patch(a_sums, r - 6)
            run(regroup_a, r - 4)
            if r - 1 != last:
                run(minima, r - 1)
            run_patch(residual, r - 6)
            normalise(r - 3)
            run(square_sums, r + 1)
            run(quantise_x, r)
            run(quantise_a, r - 5)
            run(regroup_x, r + 1)
            run_patch(residual_squares, r - 6)
        exps(last)
        reciprocals(last - 1)
        normalise_s(last - 1, NORM_S)
        warm = consts.tile([P, 1], F32)
        nc.scalar.activation(out=warm[:], in_=ones_f[:, 0:1], func=ACT.Abs_reciprocal_sqrt)
        column_sums(last - 2)
        aggregate(5)
        regroup_a(last - 2)
        normalise_v(last - 1, NORM_S, PACK)
        column_sums(last - 1)
        quantise_a(last - 3)
        a_sums(5)
        quantise_a(last - 2)
        residual(5)
        residual_squares(5)
        aggregate(6)
        reciprocals(last)
        a_sums(6)
        regroup_a(last - 1)
        normalise_v(last, 0, PACK)
        column_sums(last)
        residual(6)
        residual_squares(6)
        quantise_a(last - 1)
        regroup_a(last)
        inverse_norms(0, 7)
        a_sums(7)
        quantise_a(last)
        aggregate(7)
        residual(7)
        bounded(0, 7)
        residual_squares(7)
        inverse_norms(7, 8)
        for g in (0, 4, 1, 5, 2, 6, 3):
            accumulate(g)
        bounded(7, 8)
        accumulate(7)
